import numpy as np
import ml_dtypes


def mxq(x, axis, fmt="e4m3"):
    dtype, down = {"e4m3": (ml_dtypes.float8_e4m3fn, 7), "e5m2": (ml_dtypes.float8_e5m2, 14)}[fmt]
    v = np.moveaxis(np.asarray(x, np.float32).astype(ml_dtypes.bfloat16).astype(np.float64), axis, -1)
    blocks = v.reshape(v.shape[:-1] + (-1, 32))
    amax = np.abs(blocks).max(-1, keepdims=True)
    byte = np.maximum(np.where(amax > 0, np.frexp(amax)[1] - 1 + 127, 0) - down, 1)
    scale = np.exp2(byte - 127.0)
    codes = (blocks / scale).astype(np.float32).astype(dtype).astype(np.float64)
    return np.moveaxis((codes * scale).reshape(v.shape), -1, axis)


WIDE = False


def mx_kscale(k):
    if not WIDE:
        return np.ones(k)
    levels = np.array([10, -10, 5, -5, 0])
    a = np.random.permutation(np.resize(levels, k // 512 * 4)).reshape(k // 512, 4)
    idx = np.arange(k)
    return np.exp2(a[idx // 512, idx % 128 // 32])


BF16 = ml_dtypes.bfloat16


def bf(x):
    return np.asarray(x, np.float32).astype(BF16)


def f64(x):
    return np.asarray(x).astype(np.float64)


B, H, W, C, NH, WS, SHIFT, MR = 4, 64, 64, 256, 4, 32, 16, 4
HD = C // NH
WS2 = WS * WS
NWH, NWW = H // WS, W // WS
EPS = 1e-5
G2 = 0.1


def layer_norm(v, w, b):
    mu = v.mean(-1, keepdims=True)
    var = ((v - mu) ** 2).mean(-1, keepdims=True)
    return (v - mu) * (1.0 / np.sqrt(var + EPS)) * w + b


def setup_inputs():
    s = mx_kscale(WS2)
    u = (s / s.max()) ** 2
    um = np.tile(u.reshape(WS, WS), (NWH, NWW)).reshape(1, H * W, 1)
    d = u * np.sqrt((G2 + EPS) / (G2 * u * u + EPS))
    g = np.exp2(-7.5 * np.random.random_sample((B, H * W, 1)))
    x = (np.random.standard_normal((B, H * W, C)) + 0.5 * np.random.standard_normal((B, H * W, 1))) * g * um
    return {"x": bf(x),
            "norm1_w": bf(1.0 + 0.2 * np.random.standard_normal(C)),
            "norm1_b": bf(0.2 * np.random.standard_normal(C) * d.min()),
            "spatial_w": bf(np.random.standard_normal((NH, WS2, WS2)) / np.sqrt(WS2) / d[None, None, :]),
            "spatial_b": bf(0.3 * np.random.standard_normal((NH, WS2)))}


def reference(x, norm1_w, norm1_b, spatial_w, spatial_b):
    x = f64(x)
    xn = layer_norm(x, f64(norm1_w), f64(norm1_b))
    win = xn.reshape(B, NWH, WS, NWW, WS, C).transpose(0, 1, 3, 2, 4, 5).reshape(-1, WS2, NH, HD)
    wh = win.transpose(0, 2, 1, 3)
    out = (mxq(f64(spatial_w), 2, "e4m3")[None] @ mxq(wh, 2, "e4m3")) + f64(spatial_b)[None, :, :, None]
    w2 = out.transpose(0, 2, 1, 3).reshape(B, NWH, NWW, WS, WS, C)
    xs2 = w2.transpose(0, 1, 3, 2, 4, 5).reshape(B, H * W, C)
    return x + xs2

@@ -1,0 +1,251 @@
+from contextlib import ExitStack
+
+import concourse.mybir as mybir
+from concourse.masks import make_identity
+
+F32 = mybir.dt.float32
+BF16 = mybir.dt.bfloat16
+U32 = mybir.dt.uint32
+U8 = mybir.dt.uint8
+FP8X4 = mybir.dt.float8_e4m3fn_x4
+ALU = mybir.AluOpType
+ACT = mybir.ActivationFunctionType
+
+P = 128
+PACK = 4
+IMAGES = 4
+WINDOWS = 4
+SIDE = 32
+TOKENS = SIDE * SIDE
+PASSES = TOKENS // (P * PACK)
+CHANNELS = 256
+HALVES = CHANNELS // P
+HEADS = 4
+HEAD_DIM = CHANNELS // HEADS
+EPS = 1e-5
+COLS = WINDOWS * HEAD_DIM
+BATCH = WINDOWS * PACK
+TILES = IMAGES * PASSES * WINDOWS
+TILES_PER_IMAGE = PASSES * WINDOWS
+CHUNKS = PASSES * HEADS
+
+FLOPS = 2 * IMAGES * WINDOWS * HEADS * TOKENS * TOKENS * HEAD_DIM
+
+
+def tile_swinmlpblocknew_pa_t_kernel(tc, x, norm1_w, norm1_b, spatial_w, spatial_b, out):
+    nc = tc.nc
+
+    cut = "b (wr g r wc q j) c -> b wr wc g r q (j c)"
+    sizes = dict(wr=2, g=PASSES, r=16, wc=2, q=8, j=PACK)
+    x_cut = x.rearrange(cut, **sizes)
+    out_cut = out.rearrange(cut, **sizes)
+
+    with ExitStack() as ctx:
+        const = ctx.enter_context(tc.tile_pool(name="const", bufs=1))
+        images = ctx.enter_context(tc.tile_pool(name="images", bufs=1))
+        w_keep = ctx.enter_context(tc.tile_pool(name="w_keep", bufs=1))
+        w_stage = ctx.enter_context(tc.tile_pool(name="w_stage", bufs=2))
+        stats = ctx.enter_context(tc.tile_pool(name="stats", bufs=4))
+        norm = ctx.enter_context(tc.tile_pool(name="norm", bufs=3))
+        x_stage = ctx.enter_context(tc.tile_pool(name="x_stage", bufs=2))
+        x_keep = ctx.enter_context(tc.tile_pool(name="x_keep", bufs=2 * PASSES))
+        results = ctx.enter_context(tc.tile_pool(name="results", bufs=2))
+        turned = ctx.enter_context(tc.psum_pool(name="turned", bufs=5))
+        sums = ctx.enter_context(tc.psum_pool(name="sums", bufs=3))
+
+        x_sb = [images.tile([P, TILES_PER_IMAGE * PACK * CHANNELS], BF16, name="x_sb%d" % b) for b in range(IMAGES)]
+
+        def load_image(b):
+            rows = x_sb[b][:].rearrange("p (n g f) -> p n g f", n=WINDOWS, g=PASSES)
+            for g in range(PASSES):
+                for n in range(WINDOWS):
+                    nc.sync.dma_start(out=rows[:, n, g, :], in_=x_cut[b, n // 2, n % 2, g])
+
+        def x_tokens(b):
+            return x_sb[b][:].rearrange("p (n g j c) -> p n g j c", n=WINDOWS, g=PASSES, j=PACK)
+
+        load_image(0)
+
+        ident_f32 = const.tile([P, P], F32, name="ident_f32")
+        make_identity(nc, ident_f32[:])
+        ident_bf16 = const.tile([P, P], BF16, name="ident_bf16")
+        make_identity(nc, ident_bf16[:])
+
+        bias_rows = const.tile([P, P * PACK], BF16, name="bias_rows")
+        nc.sync.dma_start(
+            out=bias_rows[0 : HEADS * PASSES, :], in_=spatial_b.rearrange("h (g f) -> (h g) f", g=PASSES)
+        )
+        rows = const.tile([P, PACK + 1, P], BF16, name="rows")
+        nc.vector.memset(rows[:], 0.0)
+        nc.vector.tensor_copy(
+            out=rows[0 : HEADS * PASSES, 0:PACK, :],
+            in_=bias_rows[0 : HEADS * PASSES, :].rearrange("r (p j) -> r j p", j=PACK),
+        )
+        nc.sync.dma_start(out=rows[0:HALVES, PACK, :], in_=norm1_w.rearrange("(a c) -> a c", a=HALVES))
+        nc.sync.dma_start(out=rows[HALVES : 2 * HALVES, PACK, :], in_=norm1_b.rearrange("(a c) -> a c", a=HALVES))
+        rows_turned = turned.tile([P, 8, P], BF16, tag="turned", name="rows_turned")
+        for plane in range(PACK + 1):
+            nc.tensor.transpose(rows_turned[:, plane, :], rows[:, plane, :], ident_bf16[:])
+        columns = const.tile([P, PACK + 1, HEADS * PASSES], F32, name="columns")
+        nc.vector.tensor_copy(out=columns[:], in_=rows_turned[:, 0 : PACK + 1, 0 : HEADS * PASSES])
+
+        def bias_column(h, g, j):
+            return columns[:, j, PASSES * h + g : PASSES * h + g + 1]
+
+        def gain_column(half):
+            return columns[:, PACK, half : half + 1]
+
+        def shift_column(half):
+            return columns[:, PACK, HALVES + half : HALVES + half + 1]
+
+        w_codes = w_keep.tile([P, CHUNKS, PACK * PASSES * P], U32, name="w_codes", align_bytes=64)
+        w_scales = w_keep.tile([P, CHUNKS, PACK * PASSES * P], U8, name="w_scales", align_bytes=64)
+
+        def weights_chunk(k):
+            g_out, h = k // HEADS, k % HEADS
+            w_raw = w_stage.tile([P, PACK * TOKENS], BF16, name="w_raw")
+            nc.sync.dma_start(
+                out=w_raw[:],
+                in_=spatial_w[h, g_out * P * PACK : (g_out + 1) * P * PACK, :].rearrange("(p j) t -> p (j t)", j=PACK),
+            )
+            words = w_raw[:].bitcast(F32).rearrange("p (j g q u) -> p j g u q", j=PACK, g=PASSES, u=2)
+            w_grouped = w_stage.tile([P, PACK * PASSES * P * PACK], BF16, name="w_grouped", align_bytes=64)
+            grouped_words = w_grouped[:].bitcast(F32).rearrange("q (j g p u) -> q j g p u", j=PACK, g=PASSES, u=2)
+            for j in range(PACK):
+                bank = turned.tile([P, PASSES, 2, P], F32, tag="turned", name="w_bank")
+                for g in range(PASSES):
+                    for u in range(2):
+                        nc.tensor.transpose(bank[:, g, u, :], words[:, j, g, u, :], ident_f32[:])
+                nc.scalar.copy(out=grouped_words[:, j], in_=bank[:].rearrange("q g u p -> q g p u"))
+            nc.vector.quantize_mx(out=w_codes[:, k, :].bitcast(FP8X4), scales=w_scales[:, k, :], in_=w_grouped[:])
+
+        moments = {}
+
+        def batch_statistics(batch):
+            b, g = batch // PASSES, batch % PASSES
+            halves = stats.tile([P, BATCH, 6], F32, name="halves")
+            for n in range(WINDOWS):
+                for j in range(PACK):
+                    nc.vector.bn_stats(out=halves[:, PACK * n + j, :], in_=x_tokens(b)[:, n, g, j, :])
+            both = stats.tile([P, BATCH, 2], F32, name="both")
+            nc.vector.tensor_tensor(out=both[:], in0=halves[:, :, 1:3], in1=halves[:, :, 4:6], op=ALU.add)
+            gap = stats.tile([P, BATCH, 1], F32, name="gap")
+            nc.vector.tensor_tensor(out=gap[:], in0=halves[:, :, 1:2], in1=halves[:, :, 4:5], op=ALU.subtract)
+            minus_mean = stats.tile([P, BATCH, 1], F32, name="minus_mean")
+            nc.vector.tensor_scalar(out=minus_mean[:], in0=both[:, :, 0:1], scalar1=-0.5, scalar2=None, op0=ALU.mult)
+            gap_sq = stats.tile([P, BATCH, 1], F32, name="gap_sq")
+            nc.vector.tensor_tensor(out=gap_sq[:], in0=gap[:], in1=gap[:], op=ALU.mult)
+            within = stats.tile([P, BATCH, 1], F32, name="within")
+            nc.vector.tensor_scalar(
+                out=within[:], in0=both[:, :, 1:2], scalar1=1.0 / CHANNELS, scalar2=EPS, op0=ALU.mult, op1=ALU.add
+            )
+            var_eps = stats.tile([P, BATCH, 1], F32, name="var_eps")
+            nc.vector.scalar_tensor_tensor(
+                out=var_eps[:], in0=gap_sq[:], scalar=0.25, in1=within[:], op0=ALU.mult, op1=ALU.add
+            )
+            std = stats.tile([P, BATCH, 1], F32, name="std")
+            nc.scalar.activation(out=std[:], in_=var_eps[:], func=ACT.Sqrt)
+            rstd = stats.tile([P, BATCH, 1], F32, name="rstd")
+            nc.vector.reciprocal(out=rstd[:], in_=std[:])
+            moments[batch] = (minus_mean, rstd)
+
+        x_grouped = {}
+        x_codes = {}
+
+        def norm_tile(i):
+            batch, n = i // WINDOWS, i % WINDOWS
+            b, g = batch // PASSES, batch % PASSES
+            minus_mean, rstd = moments[batch]
+            x_hat = norm.tile([P, PACK, CHANNELS], F32, name="x_hat")
+            for j in range(PACK):
+                nc.gpsimd.tensor_scalar(
+                    out=x_hat[:, j, :],
+                    in0=x_tokens(b)[:, n, g, j, :],
+                    scalar1=minus_mean[:, PACK * n + j, :],
+                    scalar2=rstd[:, PACK * n + j, :],
+                    op0=ALU.add,
+                    op1=ALU.mult,
+                )
+            xn_turned = norm.tile([P, HALVES * PACK * P], BF16, name="xn_turned")
+            xn_pairs = xn_turned[:].rearrange("c (a u p e) -> c a u p e", a=HALVES, u=2, e=2)
+            for half in range(HALVES):
+                bank = turned.tile([P, PACK, P], F32, tag="turned", name="hat_bank")
+                for j in range(PACK):
+                    nc.tensor.transpose(bank[:, j, :], x_hat[:, j, half * P : (half + 1) * P], ident_f32[:])
+                nc.scalar.activation(
+                    out=xn_pairs[:, half],
+                    in_=bank[:].rearrange("c (u e) p -> c u p e", e=2),
+                    func=ACT.Identity,
+                    bias=shift_column(half),
+                    scale=gain_column(half),
+                )
+            xn_words = xn_turned[:].bitcast(F32).rearrange("c (a u p) -> c a u p", a=HALVES, u=2)
+            bank = turned.tile([P, 2, CHANNELS], F32, tag="turned", name="xn_bank")
+            for u in range(2):
+                for half in range(HALVES):
+                    nc.tensor.transpose(bank[:, u, half * P : (half + 1) * P], xn_words[:, half, u, :], ident_f32[:])
+            if n == 0:
+                x_grouped[batch] = x_stage.tile([P, HEADS * COLS * PACK], BF16, name="x_grouped", align_bytes=64)
+            grouped_words = (
+                x_grouped[batch][:].bitcast(F32).rearrange("p (h n d u) -> p h n d u", h=HEADS, n=WINDOWS, u=2)
+            )
+            nc.scalar.copy(out=grouped_words[:, :, n], in_=bank[:].rearrange("p u (h d) -> p h d u", h=HEADS))
+            if n == WINDOWS - 1:
+                codes = x_keep.tile([P, HEADS * COLS], U32, name="x_codes", align_bytes=64)
+                scales = x_keep.tile([P, HEADS * COLS], U8, name="x_scales", align_bytes=64)
+                nc.vector.quantize_mx(out=codes[:].bitcast(FP8X4), scales=scales[:], in_=x_grouped[batch][:])
+                x_codes[batch] = (codes, scales)
+
+        result = {}
+
+        def mix_unit(unit):
+            b, g_out, j = unit // TILES_PER_IMAGE, (unit % TILES_PER_IMAGE) // PACK, unit % PACK
+            if j == 0:
+                result[0] = results.tile([P, WINDOWS * PACK * CHANNELS], F32, name="result")
+            res = result[0][:].rearrange("p (n j c) -> p n j c", n=WINDOWS, j=PACK)
+            for pair in range(HEADS // 2):
+                bank = sums.tile([P, 2, COLS], F32, name="sum_bank")
+                for side in range(2):
+                    h = 2 * pair + side
+                    k = HEADS * g_out + h
+                    for g in range(PASSES):
+                        codes, scales = x_codes[PASSES * b + g]
+                        w_cols = slice((PASSES * j + g) * P, (PASSES * j + g + 1) * P)
+                        x_cols = slice(h * COLS, (h + 1) * COLS)
+                        nc.tensor.matmul_mx(
+                            out=bank[:, side, :],
+                            lhsT=w_codes[:, k, w_cols].bitcast(FP8X4),
+                            lhsT_scale=w_scales[:, k, w_cols],
+                            rhs=codes[:, x_cols].bitcast(FP8X4),
+                            rhs_scale=scales[:, x_cols],
+                            start=(g == 0),
+                            stop=(g == PASSES - 1),
+                        )
+                for side in range(2):
+                    h = 2 * pair + side
+                    channels = slice(h * HEAD_DIM, (h + 1) * HEAD_DIM)
+                    nc.vector.scalar_tensor_tensor(
+                        out=res[:, :, j, channels],
+                        in0=bank[:, side, :].rearrange("p (n d) -> p n d", n=WINDOWS),
+                        scalar=bias_column(h, g_out, j),
+                        in1=x_tokens(b)[:, :, g_out, j, channels],
+                        op0=ALU.add,
+                        op1=ALU.add,
+                    )
+            if j == PACK - 1:
+                rows_out = result[0][:].rearrange("p (n f) -> p n f", n=WINDOWS)
+                for n in range(WINDOWS):
+                    nc.sync.dma_start(out=out_cut[b, n // 2, n % 2, g_out], in_=rows_out[:, n, :])
+
+        batch_statistics(0)
+        for step in range(TILES + TILES_PER_IMAGE):
+            if step % WINDOWS == 0 and step // WINDOWS + 1 < IMAGES * PASSES:
+                batch_statistics(step // WINDOWS + 1)
+            if step < CHUNKS:
+                weights_chunk(step)
+                if step % 2 == 0 and step // 2 + 1 < IMAGES:
+                    load_image(step // 2 + 1)
+            if step < TILES:
+                norm_tile(step)
+            if step >= TILES_PER_IMAGE:
+                mix_unit(step - TILES_PER_IMAGE)

@@ -15,8 +15,7 @@ P = 128
 PACK = 4
 IMAGES = 4
 WINDOWS = 4
-SIDE = 32
-TOKENS = SIDE * SIDE
+TOKENS = 1024
 PASSES = TOKENS // (P * PACK)
 CHANNELS = 256
 HALVES = CHANNELS // P
@@ -25,9 +24,20 @@ HEAD_DIM = CHANNELS // HEADS
 EPS = 1e-5
 COLS = WINDOWS * HEAD_DIM
 BATCH = WINDOWS * PACK
-TILES = IMAGES * PASSES * WINDOWS
 TILES_PER_IMAGE = PASSES * WINDOWS
-CHUNKS = PASSES * HEADS
+TILES = IMAGES * TILES_PER_IMAGE
+UNITS = TILES
+CHUNKS = PASSES * PACK
+PSUM_BANKS = 8
+
+STATS_LEAD = 8
+TURN_LAG = 1
+BACK_LAG = 2
+QUANT_LAG = 3
+MIX_LAG = TILES_PER_IMAGE - 1 + QUANT_LAG + 1
+OUT_LAG = MIX_LAG + 1
+STEPS_PER_CHUNK = 2
+LOAD_LEAD = 4
 
 FLOPS = 2 * IMAGES * WINDOWS * HEADS * TOKENS * TOKENS * HEAD_DIM
 
@@ -46,25 +56,29 @@ def tile_swinmlpblocknew_pa_t_kernel(tc, x, norm1_w, norm1_b, spatial_w, spatial
         w_keep = ctx.enter_context(tc.tile_pool(name="w_keep", bufs=1))
         w_stage = ctx.enter_context(tc.tile_pool(name="w_stage", bufs=2))
         stats = ctx.enter_context(tc.tile_pool(name="stats", bufs=4))
-        norm = ctx.enter_context(tc.tile_pool(name="norm", bufs=3))
+        norm = ctx.enter_context(tc.tile_pool(name="norm", bufs=2))
         x_stage = ctx.enter_context(tc.tile_pool(name="x_stage", bufs=2))
         x_keep = ctx.enter_context(tc.tile_pool(name="x_keep", bufs=2 * PASSES))
         results = ctx.enter_context(tc.tile_pool(name="results", bufs=2))
-        turned = ctx.enter_context(tc.psum_pool(name="turned", bufs=5))
-        sums = ctx.enter_context(tc.psum_pool(name="sums", bufs=3))
+        banks = ctx.enter_context(tc.psum_pool(name="banks", bufs=PSUM_BANKS))
+        ctx.enter_context(tc.manual_schedule())
+
+        def place(i):
+            batch, n = i // WINDOWS, i % WINDOWS
+            return batch, batch // PASSES, batch % PASSES, n
 
         x_sb = [images.tile([P, TILES_PER_IMAGE * PACK * CHANNELS], BF16, name="x_sb%d" % b) for b in range(IMAGES)]
-
-        def load_image(b):
-            rows = x_sb[b][:].rearrange("p (n g f) -> p n g f", n=WINDOWS, g=PASSES)
-            for g in range(PASSES):
-                for n in range(WINDOWS):
-                    nc.sync.dma_start(out=rows[:, n, g, :], in_=x_cut[b, n // 2, n % 2, g])
 
         def x_tokens(b):
             return x_sb[b][:].rearrange("p (n g j c) -> p n g j c", n=WINDOWS, g=PASSES, j=PACK)
 
-        load_image(0)
+        def load_tile(i):
+            batch, b, g, n = place(i)
+            rows = x_sb[b][:].rearrange("p (n g f) -> p n g f", n=WINDOWS, g=PASSES)
+            nc.sync.dma_start(out=rows[:, n, g, :], in_=x_cut[b, n // 2, n % 2, g])
+
+        for i in range(TILES_PER_IMAGE):
+            load_tile(i)
 
         ident_f32 = const.tile([P, P], F32, name="ident_f32")
         make_identity(nc, ident_f32[:])
@@ -72,22 +86,22 @@ def tile_swinmlpblocknew_pa_t_kernel(tc, x, norm1_w, norm1_b, spatial_w, spatial
         make_identity(nc, ident_bf16[:])
 
         bias_rows = const.tile([P, P * PACK], BF16, name="bias_rows")
-        nc.sync.dma_start(
+        nc.scalar.dma_start(
             out=bias_rows[0 : HEADS * PASSES, :], in_=spatial_b.rearrange("h (g f) -> (h g) f", g=PASSES)
         )
         rows = const.tile([P, PACK + 1, P], BF16, name="rows")
-        nc.vector.memset(rows[:], 0.0)
-        nc.vector.tensor_copy(
+        nc.gpsimd.memset(rows[:], 0.0)
+        nc.scalar.dma_start(out=rows[0:HALVES, PACK, :], in_=norm1_w.rearrange("(a c) -> a c", a=HALVES))
+        nc.scalar.dma_start(out=rows[HALVES : 2 * HALVES, PACK, :], in_=norm1_b.rearrange("(a c) -> a c", a=HALVES))
+        nc.gpsimd.tensor_copy(
             out=rows[0 : HEADS * PASSES, 0:PACK, :],
             in_=bias_rows[0 : HEADS * PASSES, :].rearrange("r (p j) -> r j p", j=PACK),
         )
-        nc.sync.dma_start(out=rows[0:HALVES, PACK, :], in_=norm1_w.rearrange("(a c) -> a c", a=HALVES))
-        nc.sync.dma_start(out=rows[HALVES : 2 * HALVES, PACK, :], in_=norm1_b.rearrange("(a c) -> a c", a=HALVES))
-        rows_turned = turned.tile([P, 8, P], BF16, tag="turned", name="rows_turned")
+        rows_turned = banks.tile([P, 8, P], BF16, tag="bank", name="rows_turned")
         for plane in range(PACK + 1):
             nc.tensor.transpose(rows_turned[:, plane, :], rows[:, plane, :], ident_bf16[:])
         columns = const.tile([P, PACK + 1, HEADS * PASSES], F32, name="columns")
-        nc.vector.tensor_copy(out=columns[:], in_=rows_turned[:, 0 : PACK + 1, 0 : HEADS * PASSES])
+        nc.scalar.copy(out=columns[:], in_=rows_turned[:, 0 : PACK + 1, 0 : HEADS * PASSES])
 
         def bias_column(h, g, j):
             return columns[:, j, PASSES * h + g : PASSES * h + g + 1]
@@ -98,41 +112,54 @@ def tile_swinmlpblocknew_pa_t_kernel(tc, x, norm1_w, norm1_b, spatial_w, spatial
         def shift_column(half):
             return columns[:, PACK, HALVES + half : HALVES + half + 1]
 
-        w_codes = w_keep.tile([P, CHUNKS, PACK * PASSES * P], U32, name="w_codes", align_bytes=64)
-        w_scales = w_keep.tile([P, CHUNKS, PACK * PASSES * P], U8, name="w_scales", align_bytes=64)
+        w_codes = w_keep.tile([P, CHUNKS, HEADS * PASSES * P], U32, name="w_codes", align_bytes=64)
+        w_scales = w_keep.tile([P, CHUNKS, HEADS * PASSES * P], U8, name="w_scales", align_bytes=64)
+        w_raw = {}
+        w_grouped = {}
 
-        def weights_chunk(k):
-            g_out, h = k // HEADS, k % HEADS
-            w_raw = w_stage.tile([P, PACK * TOKENS], BF16, name="w_raw")
-            nc.sync.dma_start(
-                out=w_raw[:],
-                in_=spatial_w[h, g_out * P * PACK : (g_out + 1) * P * PACK, :].rearrange("(p j) t -> p (j t)", j=PACK),
-            )
-            words = w_raw[:].bitcast(F32).rearrange("p (j g q u) -> p j g u q", j=PACK, g=PASSES, u=2)
-            w_grouped = w_stage.tile([P, PACK * PASSES * P * PACK], BF16, name="w_grouped", align_bytes=64)
-            grouped_words = w_grouped[:].bitcast(F32).rearrange("q (j g p u) -> q j g p u", j=PACK, g=PASSES, u=2)
-            for j in range(PACK):
-                bank = turned.tile([P, PASSES, 2, P], F32, tag="turned", name="w_bank")
+        def load_weights(k):
+            g_out, j = k // PACK, k % PACK
+            w_raw[k] = w_stage.tile([P, HEADS, TOKENS], BF16, name="w_raw", bufs=3)
+            rows_of_pass = spatial_w[:, g_out * P * PACK : (g_out + 1) * P * PACK, :]
+            nc.sync.dma_start(out=w_raw[k][:], in_=rows_of_pass.rearrange("h (p j) t -> j p h t", j=PACK)[j])
+
+        def turn_weights(k, first_head):
+            if first_head == 0:
+                w_grouped[k] = w_stage.tile([P, HEADS * PASSES * P * PACK], BF16, name="w_grouped", align_bytes=64)
+            words = w_raw[k][:].bitcast(F32).rearrange("p h (g u q) -> p h g u q", g=PASSES, u=2)
+            grouped_words = w_grouped[k][:].bitcast(F32).rearrange("q (h g p u) -> q h g p u", h=HEADS, g=PASSES, u=2)
+            for h in range(first_head, first_head + HEADS // STEPS_PER_CHUNK):
+                bank = banks.tile([P, PASSES, 2, P], F32, tag="bank", name="w_bank")
                 for g in range(PASSES):
                     for u in range(2):
-                        nc.tensor.transpose(bank[:, g, u, :], words[:, j, g, u, :], ident_f32[:])
-                nc.scalar.copy(out=grouped_words[:, j], in_=bank[:].rearrange("q g u p -> q g p u"))
-            nc.vector.quantize_mx(out=w_codes[:, k, :].bitcast(FP8X4), scales=w_scales[:, k, :], in_=w_grouped[:])
+                        nc.tensor.transpose(bank[:, g, u, :], words[:, h, g, u, :], ident_f32[:])
+                nc.scalar.copy(out=grouped_words[:, h], in_=bank[:].rearrange("q g u p -> q g p u"))
 
-        moments = {}
+        def quantise_weights(k):
+            nc.vector.quantize_mx(out=w_codes[:, k, :].bitcast(FP8X4), scales=w_scales[:, k, :], in_=w_grouped[k][:])
 
-        def batch_statistics(batch):
-            b, g = batch // PASSES, batch % PASSES
-            halves = stats.tile([P, BATCH, 6], F32, name="halves")
-            for n in range(WINDOWS):
-                for j in range(PACK):
-                    nc.vector.bn_stats(out=halves[:, PACK * n + j, :], in_=x_tokens(b)[:, n, g, j, :])
+        halves = {}
+        minus_mean = {}
+        std = {}
+        rstd = {}
+
+        def tile_statistics(i):
+            batch, b, g, n = place(i)
+            if n == 0:
+                halves[batch] = stats.tile([P, BATCH, 6], F32, name="halves")
+            for j in range(PACK):
+                nc.vector.bn_stats(out=halves[batch][:, PACK * n + j, :], in_=x_tokens(b)[:, n, g, j, :])
+
+        def deviation(batch):
+            even_odd = halves[batch]
             both = stats.tile([P, BATCH, 2], F32, name="both")
-            nc.vector.tensor_tensor(out=both[:], in0=halves[:, :, 1:3], in1=halves[:, :, 4:6], op=ALU.add)
+            nc.vector.tensor_tensor(out=both[:], in0=even_odd[:, :, 1:3], in1=even_odd[:, :, 4:6], op=ALU.add)
             gap = stats.tile([P, BATCH, 1], F32, name="gap")
-            nc.vector.tensor_tensor(out=gap[:], in0=halves[:, :, 1:2], in1=halves[:, :, 4:5], op=ALU.subtract)
-            minus_mean = stats.tile([P, BATCH, 1], F32, name="minus_mean")
-            nc.vector.tensor_scalar(out=minus_mean[:], in0=both[:, :, 0:1], scalar1=-0.5, scalar2=None, op0=ALU.mult)
+            nc.vector.tensor_tensor(out=gap[:], in0=even_odd[:, :, 1:2], in1=even_odd[:, :, 4:5], op=ALU.subtract)
+            minus_mean[batch] = stats.tile([P, BATCH, 1], F32, name="minus_mean")
+            nc.vector.tensor_scalar(
+                out=minus_mean[batch][:], in0=both[:, :, 0:1], scalar1=-0.5, scalar2=None, op0=ALU.mult
+            )
             gap_sq = stats.tile([P, BATCH, 1], F32, name="gap_sq")
             nc.vector.tensor_tensor(out=gap_sq[:], in0=gap[:], in1=gap[:], op=ALU.mult)
             within = stats.tile([P, BATCH, 1], F32, name="within")
@@ -143,77 +170,81 @@ def tile_swinmlpblocknew_pa_t_kernel(tc, x, norm1_w, norm1_b, spatial_w, spatial
             nc.vector.scalar_tensor_tensor(
                 out=var_eps[:], in0=gap_sq[:], scalar=0.25, in1=within[:], op0=ALU.mult, op1=ALU.add
             )
-            std = stats.tile([P, BATCH, 1], F32, name="std")
-            nc.scalar.activation(out=std[:], in_=var_eps[:], func=ACT.Sqrt)
-            rstd = stats.tile([P, BATCH, 1], F32, name="rstd")
-            nc.vector.reciprocal(out=rstd[:], in_=std[:])
-            moments[batch] = (minus_mean, rstd)
+            std[batch] = stats.tile([P, BATCH, 1], F32, name="std")
+            nc.scalar.activation(out=std[batch][:], in_=var_eps[:], func=ACT.Sqrt)
 
+        def inverse_deviation(batch):
+            rstd[batch] = stats.tile([P, BATCH, 1], F32, name="rstd")
+            nc.vector.reciprocal(out=rstd[batch][:], in_=std[batch][:])
+
+        x_hat = {}
+        xn_turned = {}
         x_grouped = {}
         x_codes = {}
 
-        def norm_tile(i):
-            batch, n = i // WINDOWS, i % WINDOWS
-            b, g = batch // PASSES, batch % PASSES
-            minus_mean, rstd = moments[batch]
-            x_hat = norm.tile([P, PACK, CHANNELS], F32, name="x_hat")
+        def normalise(i):
+            batch, b, g, n = place(i)
+            x_hat[i] = norm.tile([P, PACK, CHANNELS], F32, name="x_hat")
             for j in range(PACK):
                 nc.gpsimd.tensor_scalar(
-                    out=x_hat[:, j, :],
+                    out=x_hat[i][:, j, :],
                     in0=x_tokens(b)[:, n, g, j, :],
-                    scalar1=minus_mean[:, PACK * n + j, :],
-                    scalar2=rstd[:, PACK * n + j, :],
+                    scalar1=minus_mean[batch][:, PACK * n + j, :],
+                    scalar2=rstd[batch][:, PACK * n + j, :],
                     op0=ALU.add,
                     op1=ALU.mult,
                 )
-            xn_turned = norm.tile([P, HALVES * PACK * P], BF16, name="xn_turned")
-            xn_pairs = xn_turned[:].rearrange("c (a u p e) -> c a u p e", a=HALVES, u=2, e=2)
+
+        def to_channels(i):
+            xn_turned[i] = norm.tile([P, HALVES, P, PACK], BF16, name="xn_turned")
             for half in range(HALVES):
-                bank = turned.tile([P, PACK, P], F32, tag="turned", name="hat_bank")
+                bank = banks.tile([P, PACK, P], F32, tag="bank", name="hat_bank")
                 for j in range(PACK):
-                    nc.tensor.transpose(bank[:, j, :], x_hat[:, j, half * P : (half + 1) * P], ident_f32[:])
+                    nc.tensor.transpose(bank[:, j, :], x_hat[i][:, j, half * P : (half + 1) * P], ident_f32[:])
                 nc.scalar.activation(
-                    out=xn_pairs[:, half],
-                    in_=bank[:].rearrange("c (u e) p -> c u p e", e=2),
+                    out=xn_turned[i][:, half],
+                    in_=bank[:].rearrange("c j p -> c p j"),
                     func=ACT.Identity,
                     bias=shift_column(half),
                     scale=gain_column(half),
                 )
-            xn_words = xn_turned[:].bitcast(F32).rearrange("c (a u p) -> c a u p", a=HALVES, u=2)
-            bank = turned.tile([P, 2, CHANNELS], F32, tag="turned", name="xn_bank")
+
+        def to_tokens(i):
+            batch, b, g, n = place(i)
+            words = xn_turned[i][:].rearrange("c a p j -> c (a p j)").bitcast(F32)
+            words = words.rearrange("c (a u q) -> c a u q", a=HALVES, u=2)
+            bank = banks.tile([P, 2, CHANNELS], F32, tag="bank", name="xn_bank")
             for u in range(2):
                 for half in range(HALVES):
-                    nc.tensor.transpose(bank[:, u, half * P : (half + 1) * P], xn_words[:, half, u, :], ident_f32[:])
+                    nc.tensor.transpose(bank[:, u, half * P : (half + 1) * P], words[:, half, u, :], ident_f32[:])
             if n == 0:
                 x_grouped[batch] = x_stage.tile([P, HEADS * COLS * PACK], BF16, name="x_grouped", align_bytes=64)
             grouped_words = (
-                x_grouped[batch][:].bitcast(F32).rearrange("p (h n d u) -> p h n d u", h=HEADS, n=WINDOWS, u=2)
+                x_grouped[batch][:].bitcast(F32).rearrange("q (h n d u) -> q h n d u", h=HEADS, n=WINDOWS, u=2)
             )
-            nc.scalar.copy(out=grouped_words[:, :, n], in_=bank[:].rearrange("p u (h d) -> p h d u", h=HEADS))
-            if n == WINDOWS - 1:
-                codes = x_keep.tile([P, HEADS * COLS], U32, name="x_codes", align_bytes=64)
-                scales = x_keep.tile([P, HEADS * COLS], U8, name="x_scales", align_bytes=64)
-                nc.vector.quantize_mx(out=codes[:].bitcast(FP8X4), scales=scales[:], in_=x_grouped[batch][:])
-                x_codes[batch] = (codes, scales)
+            nc.scalar.copy(out=grouped_words[:, :, n], in_=bank[:].rearrange("q u (h d) -> q h d u", h=HEADS))
 
+        def quantise_tokens(batch):
+            codes = x_keep.tile([P, HEADS * COLS], U32, name="x_codes", align_bytes=64)
+            scales = x_keep.tile([P, HEADS * COLS], U8, name="x_scales", align_bytes=64)
+            nc.vector.quantize_mx(out=codes[:].bitcast(FP8X4), scales=scales[:], in_=x_grouped[batch][:])
+            x_codes[batch] = (codes, scales)
+
+        sums = {}
         result = {}
 
-        def mix_unit(unit):
-            b, g_out, j = unit // TILES_PER_IMAGE, (unit % TILES_PER_IMAGE) // PACK, unit % PACK
-            if j == 0:
-                result[0] = results.tile([P, WINDOWS * PACK * CHANNELS], F32, name="result")
-            res = result[0][:].rearrange("p (n j c) -> p n j c", n=WINDOWS, j=PACK)
+        def multiply(unit):
+            b, k = unit // CHUNKS, unit % CHUNKS
             for pair in range(HEADS // 2):
-                bank = sums.tile([P, 2, COLS], F32, name="sum_bank")
+                sums[unit, pair] = banks.tile([P, 2, COLS], F32, tag="bank", name="sum_bank")
                 for side in range(2):
                     h = 2 * pair + side
-                    k = HEADS * g_out + h
                     for g in range(PASSES):
                         codes, scales = x_codes[PASSES * b + g]
-                        w_cols = slice((PASSES * j + g) * P, (PASSES * j + g + 1) * P)
+                        w_cols = slice((PASSES * h + g) * P, (PASSES * h + g + 1) * P)
                         x_cols = slice(h * COLS, (h + 1) * COLS)
                         nc.tensor.matmul_mx(
-                            out=bank[:, side, :],
+                            out=sums[unit, pair][:, side, :],
                             lhsT=w_codes[:, k, w_cols].bitcast(FP8X4),
                             lhsT_scale=w_scales[:, k, w_cols],
                             rhs=codes[:, x_cols].bitcast(FP8X4),
@@ -221,31 +252,57 @@ def tile_swinmlpblocknew_pa_t_kernel(tc, x, norm1_w, norm1_b, spatial_w, spatial
                             start=(g == 0),
                             stop=(g == PASSES - 1),
                         )
-                for side in range(2):
-                    h = 2 * pair + side
-                    channels = slice(h * HEAD_DIM, (h + 1) * HEAD_DIM)
-                    nc.vector.scalar_tensor_tensor(
-                        out=res[:, :, j, channels],
-                        in0=bank[:, side, :].rearrange("p (n d) -> p n d", n=WINDOWS),
-                        scalar=bias_column(h, g_out, j),
-                        in1=x_tokens(b)[:, :, g_out, j, channels],
-                        op0=ALU.add,
-                        op1=ALU.add,
-                    )
-            if j == PACK - 1:
-                rows_out = result[0][:].rearrange("p (n f) -> p n f", n=WINDOWS)
-                for n in range(WINDOWS):
-                    nc.sync.dma_start(out=out_cut[b, n // 2, n % 2, g_out], in_=rows_out[:, n, :])
 
-        batch_statistics(0)
-        for step in range(TILES + TILES_PER_IMAGE):
-            if step % WINDOWS == 0 and step // WINDOWS + 1 < IMAGES * PASSES:
-                batch_statistics(step // WINDOWS + 1)
-            if step < CHUNKS:
-                weights_chunk(step)
-                if step % 2 == 0 and step // 2 + 1 < IMAGES:
-                    load_image(step // 2 + 1)
-            if step < TILES:
-                norm_tile(step)
-            if step >= TILES_PER_IMAGE:
-                mix_unit(step - TILES_PER_IMAGE)
+        def add_and_store(unit):
+            b, k = unit // CHUNKS, unit % CHUNKS
+            g_out, j = k // PACK, k % PACK
+            if j == 0:
+                result[b, g_out] = results.tile([P, WINDOWS, PACK, CHANNELS], F32, name="result")
+            res = result[b, g_out]
+            for h in range(HEADS):
+                channels = slice(h * HEAD_DIM, (h + 1) * HEAD_DIM)
+                nc.vector.scalar_tensor_tensor(
+                    out=res[:, :, j, channels],
+                    in0=sums[unit, h // 2][:, h % 2, :].rearrange("p (n d) -> p n d", n=WINDOWS),
+                    scalar=bias_column(h, g_out, j),
+                    in1=x_tokens(b)[:, :, g_out, j, channels],
+                    op0=ALU.add,
+                    op1=ALU.add,
+                )
+            if j == PACK - 1:
+                for n in range(WINDOWS):
+                    nc.sync.dma_start(
+                        out=out_cut[b, n // 2, n % 2, g_out], in_=res[:, n].rearrange("p j c -> p (j c)")
+                    )
+
+        def last_of_batch(i):
+            return 0 <= i < TILES and i % WINDOWS == WINDOWS - 1
+
+        for step in range(-STATS_LEAD, UNITS + OUT_LAG):
+            if last_of_batch(step + STATS_LEAD - 1):
+                inverse_deviation((step + STATS_LEAD - 1) // WINDOWS)
+            if 0 <= step - OUT_LAG:
+                add_and_store(step - OUT_LAG)
+            if last_of_batch(step - QUANT_LAG):
+                quantise_tokens((step - QUANT_LAG) // WINDOWS)
+            if step % STEPS_PER_CHUNK == 0 and 0 <= step // STEPS_PER_CHUNK - 1 < CHUNKS:
+                quantise_weights(step // STEPS_PER_CHUNK - 1)
+            if 0 <= step - BACK_LAG < TILES:
+                to_tokens(step - BACK_LAG)
+            if 0 <= step - TURN_LAG < TILES:
+                to_channels(step - TURN_LAG)
+            if 0 <= step < CHUNKS * STEPS_PER_CHUNK:
+                turn_weights(step // STEPS_PER_CHUNK, (step % STEPS_PER_CHUNK) * (HEADS // STEPS_PER_CHUNK))
+            if 0 <= step - MIX_LAG < UNITS:
+                multiply(step - MIX_LAG)
+            if 0 <= step < TILES:
+                normalise(step)
+            if step + STATS_LEAD < TILES:
+                tile_statistics(step + STATS_LEAD)
+                if last_of_batch(step + STATS_LEAD):
+                    deviation((step + STATS_LEAD) // WINDOWS)
+            group = (step + LOAD_LEAD) // STEPS_PER_CHUNK
+            if (step + LOAD_LEAD) % STEPS_PER_CHUNK == 0 and 0 <= group < CHUNKS:
+                load_weights(group)
+                for i in range(TILES_PER_IMAGE + WINDOWS * group, min(TILES_PER_IMAGE + WINDOWS * (group + 1), TILES)):
+                    load_tile(i)

@@ -27,17 +27,19 @@ BATCH = WINDOWS * PACK
 TILES_PER_IMAGE = PASSES * WINDOWS
 TILES = IMAGES * TILES_PER_IMAGE
 UNITS = TILES
-CHUNKS = PASSES * PACK
+KINDS = PASSES * PACK
+PAIRS = HEADS // 2
+CHUNKS = KINDS * PAIRS
 PSUM_BANKS = 8
 
 STATS_LEAD = 8
 TURN_LAG = 1
-BACK_LAG = 2
-QUANT_LAG = 3
+BACK_LAG = 3
+QUANT_LAG = BACK_LAG + 1
 MIX_LAG = TILES_PER_IMAGE - 1 + QUANT_LAG + 1
 OUT_LAG = MIX_LAG + 1
-STEPS_PER_CHUNK = 2
 LOAD_LEAD = 4
+TILES_PER_LOAD = 2
 
 FLOPS = 2 * IMAGES * WINDOWS * HEADS * TOKENS * TOKENS * HEAD_DIM
 
@@ -56,7 +58,7 @@ def tile_swinmlpblocknew_pa_t_kernel(tc, x, norm1_w, norm1_b, spatial_w, spatial
         w_keep = ctx.enter_context(tc.tile_pool(name="w_keep", bufs=1))
         w_stage = ctx.enter_context(tc.tile_pool(name="w_stage", bufs=2))
         stats = ctx.enter_context(tc.tile_pool(name="stats", bufs=4))
-        norm = ctx.enter_context(tc.tile_pool(name="norm", bufs=2))
+        norm = ctx.enter_context(tc.tile_pool(name="norm", bufs=3))
         x_stage = ctx.enter_context(tc.tile_pool(name="x_stage", bufs=2))
         x_keep = ctx.enter_context(tc.tile_pool(name="x_keep", bufs=2 * PASSES))
         results = ctx.enter_context(tc.tile_pool(name="results", bufs=2))
@@ -112,34 +114,37 @@ def tile_swinmlpblocknew_pa_t_kernel(tc, x, norm1_w, norm1_b, spatial_w, spatial
         def shift_column(half):
             return columns[:, PACK, HALVES + half : HALVES + half + 1]
 
-        w_codes = w_keep.tile([P, CHUNKS, HEADS * PASSES * P], U32, name="w_codes", align_bytes=64)
-        w_scales = w_keep.tile([P, CHUNKS, HEADS * PASSES * P], U8, name="w_scales", align_bytes=64)
+        w_codes = w_keep.tile([P, CHUNKS, 2 * PASSES * P], U32, name="w_codes", align_bytes=64)
+        w_scales = w_keep.tile([P, CHUNKS, 2 * PASSES * P], U8, name="w_scales", align_bytes=64)
         w_raw = {}
         w_grouped = {}
 
-        def load_weights(k):
-            g_out, j = k // PACK, k % PACK
-            w_raw[k] = w_stage.tile([P, HEADS, TOKENS], BF16, name="w_raw", bufs=3)
-            rows_of_pass = spatial_w[:, g_out * P * PACK : (g_out + 1) * P * PACK, :]
-            nc.sync.dma_start(out=w_raw[k][:], in_=rows_of_pass.rearrange("h (p j) t -> j p h t", j=PACK)[j])
+        def load_weights(chunk):
+            kind, pair = chunk // PAIRS, chunk % PAIRS
+            g_out, j = kind // PACK, kind % PACK
+            w_raw[chunk] = w_stage.tile([P, 2, TOKENS], BF16, name="w_raw", bufs=LOAD_LEAD)
+            rows_of_pass = spatial_w[2 * pair : 2 * pair + 2, g_out * P * PACK : (g_out + 1) * P * PACK, :]
+            nc.sync.dma_start(out=w_raw[chunk][:], in_=rows_of_pass.rearrange("h (p j) t -> j p h t", j=PACK)[j])
 
-        def turn_weights(k, first_head):
-            if first_head == 0:
-                w_grouped[k] = w_stage.tile([P, HEADS * PASSES * P * PACK], BF16, name="w_grouped", align_bytes=64)
-            words = w_raw[k][:].bitcast(F32).rearrange("p h (g u q) -> p h g u q", g=PASSES, u=2)
-            grouped_words = w_grouped[k][:].bitcast(F32).rearrange("q (h g p u) -> q h g p u", h=HEADS, g=PASSES, u=2)
-            for h in range(first_head, first_head + HEADS // STEPS_PER_CHUNK):
+        def turn_weights(chunk):
+            w_grouped[chunk] = w_stage.tile([P, 2 * PASSES * P * PACK], BF16, name="w_grouped", align_bytes=64)
+            words = w_raw[chunk][:].bitcast(F32).rearrange("p h (g u q) -> p h g u q", g=PASSES, u=2)
+            grouped_words = w_grouped[chunk][:].bitcast(F32).rearrange("q (h g p u) -> q h g p u", h=2, g=PASSES, u=2)
+            for side in range(2):
                 bank = banks.tile([P, PASSES, 2, P], F32, tag="bank", name="w_bank")
                 for g in range(PASSES):
                     for u in range(2):
-                        nc.tensor.transpose(bank[:, g, u, :], words[:, h, g, u, :], ident_f32[:])
-                nc.scalar.copy(out=grouped_words[:, h], in_=bank[:].rearrange("q g u p -> q g p u"))
+                        nc.tensor.transpose(bank[:, g, u, :], words[:, side, g, u, :], ident_f32[:])
+                nc.scalar.copy(out=grouped_words[:, side], in_=bank[:].rearrange("q g u p -> q g p u"))
 
-        def quantise_weights(k):
-            nc.vector.quantize_mx(out=w_codes[:, k, :].bitcast(FP8X4), scales=w_scales[:, k, :], in_=w_grouped[k][:])
+        def quantise_weights(chunk):
+            nc.vector.quantize_mx(
+                out=w_codes[:, chunk, :].bitcast(FP8X4), scales=w_scales[:, chunk, :], in_=w_grouped[chunk][:]
+            )
 
         halves = {}
         minus_mean = {}
+        variance = {}
         std = {}
         rstd = {}
 
@@ -170,8 +175,11 @@ def tile_swinmlpblocknew_pa_t_kernel(tc, x, norm1_w, norm1_b, spatial_w, spatial
             nc.vector.scalar_tensor_tensor(
                 out=var_eps[:], in0=gap_sq[:], scalar=0.25, in1=within[:], op0=ALU.mult, op1=ALU.add
             )
+            variance[batch] = var_eps
+
+        def root(batch):
             std[batch] = stats.tile([P, BATCH, 1], F32, name="std")
-            nc.scalar.activation(out=std[batch][:], in_=var_eps[:], func=ACT.Sqrt)
+            nc.scalar.activation(out=std[batch][:], in_=variance[batch][:], func=ACT.Sqrt)
 
         def inverse_deviation(batch):
             rstd[batch] = stats.tile([P, BATCH, 1], F32, name="rstd")
@@ -234,19 +242,20 @@ def tile_swinmlpblocknew_pa_t_kernel(tc, x, norm1_w, norm1_b, spatial_w, spatial
         result = {}
 
         def multiply(unit):
-            b, k = unit // CHUNKS, unit % CHUNKS
-            for pair in range(HEADS // 2):
+            b, kind = unit // KINDS, unit % KINDS
+            for pair in range(PAIRS):
+                chunk = PAIRS * kind + pair
                 sums[unit, pair] = banks.tile([P, 2, COLS], F32, tag="bank", name="sum_bank")
                 for side in range(2):
                     h = 2 * pair + side
                     for g in range(PASSES):
                         codes, scales = x_codes[PASSES * b + g]
-                        w_cols = slice((PASSES * h + g) * P, (PASSES * h + g + 1) * P)
+                        w_cols = slice((PASSES * side + g) * P, (PASSES * side + g + 1) * P)
                         x_cols = slice(h * COLS, (h + 1) * COLS)
                         nc.tensor.matmul_mx(
                             out=sums[unit, pair][:, side, :],
-                            lhsT=w_codes[:, k, w_cols].bitcast(FP8X4),
-                            lhsT_scale=w_scales[:, k, w_cols],
+                            lhsT=w_codes[:, chunk, w_cols].bitcast(FP8X4),
+                            lhsT_scale=w_scales[:, chunk, w_cols],
                             rhs=codes[:, x_cols].bitcast(FP8X4),
                             rhs_scale=scales[:, x_cols],
                             start=(g == 0),
@@ -254,8 +263,8 @@ def tile_swinmlpblocknew_pa_t_kernel(tc, x, norm1_w, norm1_b, spatial_w, spatial
                         )
 
         def add_and_store(unit):
-            b, k = unit // CHUNKS, unit % CHUNKS
-            g_out, j = k // PACK, k % PACK
+            b, kind = unit // KINDS, unit % KINDS
+            g_out, j = kind // PACK, kind % PACK
             if j == 0:
                 result[b, g_out] = results.tile([P, WINDOWS, PACK, CHANNELS], F32, name="result")
             res = result[b, g_out]
@@ -279,20 +288,22 @@ def tile_swinmlpblocknew_pa_t_kernel(tc, x, norm1_w, norm1_b, spatial_w, spatial
             return 0 <= i < TILES and i % WINDOWS == WINDOWS - 1
 
         for step in range(-STATS_LEAD, UNITS + OUT_LAG):
-            if last_of_batch(step + STATS_LEAD - 1):
-                inverse_deviation((step + STATS_LEAD - 1) // WINDOWS)
+            if last_of_batch(step + STATS_LEAD - 2):
+                inverse_deviation((step + STATS_LEAD - 2) // WINDOWS)
             if 0 <= step - OUT_LAG:
                 add_and_store(step - OUT_LAG)
             if last_of_batch(step - QUANT_LAG):
                 quantise_tokens((step - QUANT_LAG) // WINDOWS)
-            if step % STEPS_PER_CHUNK == 0 and 0 <= step // STEPS_PER_CHUNK - 1 < CHUNKS:
-                quantise_weights(step // STEPS_PER_CHUNK - 1)
+            if 0 <= step - 1 < CHUNKS:
+                quantise_weights(step - 1)
+            if last_of_batch(step + STATS_LEAD - 1):
+                root((step + STATS_LEAD - 1) // WINDOWS)
             if 0 <= step - BACK_LAG < TILES:
                 to_tokens(step - BACK_LAG)
             if 0 <= step - TURN_LAG < TILES:
                 to_channels(step - TURN_LAG)
-            if 0 <= step < CHUNKS * STEPS_PER_CHUNK:
-                turn_weights(step // STEPS_PER_CHUNK, (step % STEPS_PER_CHUNK) * (HEADS // STEPS_PER_CHUNK))
+            if 0 <= step < CHUNKS:
+                turn_weights(step)
             if 0 <= step - MIX_LAG < UNITS:
                 multiply(step - MIX_LAG)
             if 0 <= step < TILES:
@@ -301,8 +312,9 @@ def tile_swinmlpblocknew_pa_t_kernel(tc, x, norm1_w, norm1_b, spatial_w, spatial
                 tile_statistics(step + STATS_LEAD)
                 if last_of_batch(step + STATS_LEAD):
                     deviation((step + STATS_LEAD) // WINDOWS)
-            group = (step + LOAD_LEAD) // STEPS_PER_CHUNK
-            if (step + LOAD_LEAD) % STEPS_PER_CHUNK == 0 and 0 <= group < CHUNKS:
-                load_weights(group)
-                for i in range(TILES_PER_IMAGE + WINDOWS * group, min(TILES_PER_IMAGE + WINDOWS * (group + 1), TILES)):
+            chunk = step + LOAD_LEAD
+            if 0 <= chunk < CHUNKS:
+                load_weights(chunk)
+                first = TILES_PER_IMAGE + TILES_PER_LOAD * chunk
+                for i in range(first, min(first + TILES_PER_LOAD, TILES)):
                     load_tile(i)

@@ -32,7 +32,7 @@ PAIRS = HEADS // 2
 CHUNKS = KINDS * PAIRS
 PSUM_BANKS = 8
 
-STATS_LEAD = 8
+STATS_LEAD = 6
 TURN_LAG = 1
 BACK_LAG = 3
 QUANT_LAG = BACK_LAG + 1
@@ -161,15 +161,15 @@ def tile_swinmlpblocknew_pa_t_kernel(tc, x, norm1_w, norm1_b, spatial_w, spatial
             nc.vector.tensor_tensor(out=both[:], in0=even_odd[:, :, 1:3], in1=even_odd[:, :, 4:6], op=ALU.add)
             gap = stats.tile([P, BATCH, 1], F32, name="gap")
             nc.vector.tensor_tensor(out=gap[:], in0=even_odd[:, :, 1:2], in1=even_odd[:, :, 4:5], op=ALU.subtract)
-            minus_mean[batch] = stats.tile([P, BATCH, 1], F32, name="minus_mean")
-            nc.vector.tensor_scalar(
-                out=minus_mean[batch][:], in0=both[:, :, 0:1], scalar1=-0.5, scalar2=None, op0=ALU.mult
-            )
-            gap_sq = stats.tile([P, BATCH, 1], F32, name="gap_sq")
-            nc.vector.tensor_tensor(out=gap_sq[:], in0=gap[:], in1=gap[:], op=ALU.mult)
             within = stats.tile([P, BATCH, 1], F32, name="within")
             nc.vector.tensor_scalar(
                 out=within[:], in0=both[:, :, 1:2], scalar1=1.0 / CHANNELS, scalar2=EPS, op0=ALU.mult, op1=ALU.add
+            )
+            gap_sq = stats.tile([P, BATCH, 1], F32, name="gap_sq")
+            nc.vector.tensor_tensor(out=gap_sq[:], in0=gap[:], in1=gap[:], op=ALU.mult)
+            minus_mean[batch] = stats.tile([P, BATCH, 1], F32, name="minus_mean")
+            nc.vector.tensor_scalar(
+                out=minus_mean[batch][:], in0=both[:, :, 0:1], scalar1=-0.5, scalar2=None, op0=ALU.mult
             )
             var_eps = stats.tile([P, BATCH, 1], F32, name="var_eps")
             nc.vector.scalar_tensor_tensor(
@@ -194,7 +194,7 @@ def tile_swinmlpblocknew_pa_t_kernel(tc, x, norm1_w, norm1_b, spatial_w, spatial
             batch, b, g, n = place(i)
             x_hat[i] = norm.tile([P, PACK, CHANNELS], F32, name="x_hat")
             for j in range(PACK):
-                nc.gpsimd.tensor_scalar(
+                nc.vector.tensor_scalar(
                     out=x_hat[i][:, j, :],
                     in0=x_tokens(b)[:, n, g, j, :],
                     scalar1=minus_mean[batch][:, PACK * n + j, :],

from contextlib import ExitStack

import concourse.mybir as mybir
from concourse.masks import make_identity

F32 = mybir.dt.float32
BF16 = mybir.dt.bfloat16
U32 = mybir.dt.uint32
U8 = mybir.dt.uint8
FP8X4 = mybir.dt.float8_e4m3fn_x4
ALU = mybir.AluOpType
ACT = mybir.ActivationFunctionType

P = 128
PACK = 4
IMAGES = 4
WINDOWS = 4
TOKENS = 1024
PASSES = TOKENS // (P * PACK)
CHANNELS = 256
HALVES = CHANNELS // P
HEADS = 4
HEAD_DIM = CHANNELS // HEADS
EPS = 1e-5
COLS = WINDOWS * HEAD_DIM
BATCH = WINDOWS * PACK
TILES_PER_IMAGE = PASSES * WINDOWS
TILES = IMAGES * TILES_PER_IMAGE
UNITS = TILES
KINDS = PASSES * PACK
PAIRS = HEADS // 2
CHUNKS = KINDS * PAIRS
PSUM_BANKS = 8

STATS_LEAD = 6
TURN_LAG = 1
BACK_LAG = 3
QUANT_LAG = BACK_LAG + 1
MIX_LAG = TILES_PER_IMAGE - 1 + QUANT_LAG + 1
OUT_LAG = MIX_LAG + 1
LOAD_LEAD = 4
TILES_PER_LOAD = 2

FLOPS = 2 * IMAGES * WINDOWS * HEADS * TOKENS * TOKENS * HEAD_DIM


def tile_swinmlpblocknew_pa_t_kernel(tc, x, norm1_w, norm1_b, spatial_w, spatial_b, out):
    nc = tc.nc

    cut = "b (wr g r wc q j) c -> b wr wc g r q (j c)"
    sizes = dict(wr=2, g=PASSES, r=16, wc=2, q=8, j=PACK)
    x_cut = x.rearrange(cut, **sizes)
    out_cut = out.rearrange(cut, **sizes)

    with ExitStack() as ctx:
        const = ctx.enter_context(tc.tile_pool(name="const", bufs=1))
        images = ctx.enter_context(tc.tile_pool(name="images", bufs=1))
        w_keep = ctx.enter_context(tc.tile_pool(name="w_keep", bufs=1))
        w_stage = ctx.enter_context(tc.tile_pool(name="w_stage", bufs=2))
        stats = ctx.enter_context(tc.tile_pool(name="stats", bufs=4))
        norm = ctx.enter_context(tc.tile_pool(name="norm", bufs=3))
        x_stage = ctx.enter_context(tc.tile_pool(name="x_stage", bufs=2))
        x_keep = ctx.enter_context(tc.tile_pool(name="x_keep", bufs=2 * PASSES))
        results = ctx.enter_context(tc.tile_pool(name="results", bufs=2))
        banks = ctx.enter_context(tc.psum_pool(name="banks", bufs=PSUM_BANKS))
        ctx.enter_context(tc.manual_schedule())

        def place(i):
            batch, n = i // WINDOWS, i % WINDOWS
            return batch, batch // PASSES, batch % PASSES, n

        x_sb = [images.tile([P, TILES_PER_IMAGE * PACK * CHANNELS], BF16, name="x_sb%d" % b) for b in range(IMAGES)]

        def x_tokens(b):
            return x_sb[b][:].rearrange("p (n g j c) -> p n g j c", n=WINDOWS, g=PASSES, j=PACK)

        def load_tile(i):
            batch, b, g, n = place(i)
            rows = x_sb[b][:].rearrange("p (n g f) -> p n g f", n=WINDOWS, g=PASSES)
            nc.sync.dma_start(out=rows[:, n, g, :], in_=x_cut[b, n // 2, n % 2, g])

        for i in range(TILES_PER_IMAGE):
            load_tile(i)

        ident_f32 = const.tile([P, P], F32, name="ident_f32")
        make_identity(nc, ident_f32[:])
        ident_bf16 = const.tile([P, P], BF16, name="ident_bf16")
        make_identity(nc, ident_bf16[:])

        bias_rows = const.tile([P, P * PACK], BF16, name="bias_rows")
        nc.scalar.dma_start(
            out=bias_rows[0 : HEADS * PASSES, :], in_=spatial_b.rearrange("h (g f) -> (h g) f", g=PASSES)
        )
        rows = const.tile([P, PACK + 1, P], BF16, name="rows")
        nc.gpsimd.memset(rows[:], 0.0)
        nc.scalar.dma_start(out=rows[0:HALVES, PACK, :], in_=norm1_w.rearrange("(a c) -> a c", a=HALVES))
        nc.scalar.dma_start(out=rows[HALVES : 2 * HALVES, PACK, :], in_=norm1_b.rearrange("(a c) -> a c", a=HALVES))
        nc.gpsimd.tensor_copy(
            out=rows[0 : HEADS * PASSES, 0:PACK, :],
            in_=bias_rows[0 : HEADS * PASSES, :].rearrange("r (p j) -> r j p", j=PACK),
        )
        rows_turned = banks.tile([P, 8, P], BF16, tag="bank", name="rows_turned")
        for plane in range(PACK + 1):
            nc.tensor.transpose(rows_turned[:, plane, :], rows[:, plane, :], ident_bf16[:])
        columns = const.tile([P, PACK + 1, HEADS * PASSES], F32, name="columns")
        nc.scalar.copy(out=columns[:], in_=rows_turned[:, 0 : PACK + 1, 0 : HEADS * PASSES])

        def bias_column(h, g, j):
            return columns[:, j, PASSES * h + g : PASSES * h + g + 1]

        def gain_column(half):
            return columns[:, PACK, half : half + 1]

        def shift_column(half):
            return columns[:, PACK, HALVES + half : HALVES + half + 1]

        w_codes = w_keep.tile([P, CHUNKS, 2 * PASSES * P], U32, name="w_codes", align_bytes=64)
        w_scales = w_keep.tile([P, CHUNKS, 2 * PASSES * P], U8, name="w_scales", align_bytes=64)
        w_raw = {}
        w_grouped = {}

        def load_weights(chunk):
            kind, pair = chunk // PAIRS, chunk % PAIRS
            g_out, j = kind // PACK, kind % PACK
            w_raw[chunk] = w_stage.tile([P, 2, TOKENS], BF16, name="w_raw", bufs=LOAD_LEAD)
            rows_of_pass = spatial_w[2 * pair : 2 * pair + 2, g_out * P * PACK : (g_out + 1) * P * PACK, :]
            nc.sync.dma_start(out=w_raw[chunk][:], in_=rows_of_pass.rearrange("h (p j) t -> j p h t", j=PACK)[j])

        def turn_weights(chunk):
            w_grouped[chunk] = w_stage.tile([P, 2 * PASSES * P * PACK], BF16, name="w_grouped", align_bytes=64)
            words = w_raw[chunk][:].bitcast(F32).rearrange("p h (g u q) -> p h g u q", g=PASSES, u=2)
            grouped_words = w_grouped[chunk][:].bitcast(F32).rearrange("q (h g p u) -> q h g p u", h=2, g=PASSES, u=2)
            for side in range(2):
                bank = banks.tile([P, PASSES, 2, P], F32, tag="bank", name="w_bank")
                for g in range(PASSES):
                    for u in range(2):
                        nc.tensor.transpose(bank[:, g, u, :], words[:, side, g, u, :], ident_f32[:])
                nc.scalar.copy(out=grouped_words[:, side], in_=bank[:].rearrange("q g u p -> q g p u"))

        def quantise_weights(chunk):
            nc.vector.quantize_mx(
                out=w_codes[:, chunk, :].bitcast(FP8X4), scales=w_scales[:, chunk, :], in_=w_grouped[chunk][:]
            )

        halves = {}
        minus_mean = {}
        variance = {}
        std = {}
        rstd = {}

        def tile_statistics(i):
            batch, b, g, n = place(i)
            if n == 0:
                halves[batch] = stats.tile([P, BATCH, 6], F32, name="halves")
            for j in range(PACK):
                nc.vector.bn_stats(out=halves[batch][:, PACK * n + j, :], in_=x_tokens(b)[:, n, g, j, :])

        def deviation(batch):
            even_odd = halves[batch]
            both = stats.tile([P, BATCH, 2], F32, name="both")
            nc.vector.tensor_tensor(out=both[:], in0=even_odd[:, :, 1:3], in1=even_odd[:, :, 4:6], op=ALU.add)
            gap = stats.tile([P, BATCH, 1], F32, name="gap")
            nc.vector.tensor_tensor(out=gap[:], in0=even_odd[:, :, 1:2], in1=even_odd[:, :, 4:5], op=ALU.subtract)
            within = stats.tile([P, BATCH, 1], F32, name="within")
            nc.vector.tensor_scalar(
                out=within[:], in0=both[:, :, 1:2], scalar1=1.0 / CHANNELS, scalar2=EPS, op0=ALU.mult, op1=ALU.add
            )
            gap_sq = stats.tile([P, BATCH, 1], F32, name="gap_sq")
            nc.vector.tensor_tensor(out=gap_sq[:], in0=gap[:], in1=gap[:], op=ALU.mult)
            minus_mean[batch] = stats.tile([P, BATCH, 1], F32, name="minus_mean")
            nc.vector.tensor_scalar(
                out=minus_mean[batch][:], in0=both[:, :, 0:1], scalar1=-0.5, scalar2=None, op0=ALU.mult
            )
            var_eps = stats.tile([P, BATCH, 1], F32, name="var_eps")
            nc.vector.scalar_tensor_tensor(
                out=var_eps[:], in0=gap_sq[:], scalar=0.25, in1=within[:], op0=ALU.mult, op1=ALU.add
            )
            variance[batch] = var_eps

        def root(batch):
            std[batch] = stats.tile([P, BATCH, 1], F32, name="std")
            nc.scalar.activation(out=std[batch][:], in_=variance[batch][:], func=ACT.Sqrt)

        def inverse_deviation(batch):
            rstd[batch] = stats.tile([P, BATCH, 1], F32, name="rstd")
            nc.vector.reciprocal(out=rstd[batch][:], in_=std[batch][:])

        x_hat = {}
        xn_turned = {}
        x_grouped = {}
        x_codes = {}

        def normalise(i):
            batch, b, g, n = place(i)
            x_hat[i] = norm.tile([P, PACK, CHANNELS], F32, name="x_hat")
            for j in range(PACK):
                nc.vector.tensor_scalar(
                    out=x_hat[i][:, j, :],
                    in0=x_tokens(b)[:, n, g, j, :],
                    scalar1=minus_mean[batch][:, PACK * n + j, :],
                    scalar2=rstd[batch][:, PACK * n + j, :],
                    op0=ALU.add,
                    op1=ALU.mult,
                )

        def to_channels(i):
            xn_turned[i] = norm.tile([P, HALVES, P, PACK], BF16, name="xn_turned")
            for half in range(HALVES):
                bank = banks.tile([P, PACK, P], F32, tag="bank", name="hat_bank")
                for j in range(PACK):
                    nc.tensor.transpose(bank[:, j, :], x_hat[i][:, j, half * P : (half + 1) * P], ident_f32[:])
                nc.scalar.activation(
                    out=xn_turned[i][:, half],
                    in_=bank[:].rearrange("c j p -> c p j"),
                    func=ACT.Identity,
                    bias=shift_column(half),
                    scale=gain_column(half),
                )

        def to_tokens(i):
            batch, b, g, n = place(i)
            words = xn_turned[i][:].rearrange("c a p j -> c (a p j)").bitcast(F32)
            words = words.rearrange("c (a u q) -> c a u q", a=HALVES, u=2)
            bank = banks.tile([P, 2, CHANNELS], F32, tag="bank", name="xn_bank")
            for u in range(2):
                for half in range(HALVES):
                    nc.tensor.transpose(bank[:, u, half * P : (half + 1) * P], words[:, half, u, :], ident_f32[:])
            if n == 0:
                x_grouped[batch] = x_stage.tile([P, HEADS * COLS * PACK], BF16, name="x_grouped", align_bytes=64)
            grouped_words = (
                x_grouped[batch][:].bitcast(F32).rearrange("q (h n d u) -> q h n d u", h=HEADS, n=WINDOWS, u=2)
            )
            nc.scalar.copy(out=grouped_words[:, :, n], in_=bank[:].rearrange("q u (h d) -> q h d u", h=HEADS))

        def quantise_tokens(batch):
            codes = x_keep.tile([P, HEADS * COLS], U32, name="x_codes", align_bytes=64)
            scales = x_keep.tile([P, HEADS * COLS], U8, name="x_scales", align_bytes=64)
            nc.vector.quantize_mx(out=codes[:].bitcast(FP8X4), scales=scales[:], in_=x_grouped[batch][:])
            x_codes[batch] = (codes, scales)

        sums = {}
        result = {}

        def multiply(unit):
            b, kind = unit // KINDS, unit % KINDS
            for pair in range(PAIRS):
                chunk = PAIRS * kind + pair
                sums[unit, pair] = banks.tile([P, 2, COLS], F32, tag="bank", name="sum_bank")
                for side in range(2):
                    h = 2 * pair + side
                    for g in range(PASSES):
                        codes, scales = x_codes[PASSES * b + g]
                        w_cols = slice((PASSES * side + g) * P, (PASSES * side + g + 1) * P)
                        x_cols = slice(h * COLS, (h + 1) * COLS)
                        nc.tensor.matmul_mx(
                            out=sums[unit, pair][:, side, :],
                            lhsT=w_codes[:, chunk, w_cols].bitcast(FP8X4),
                            lhsT_scale=w_scales[:, chunk, w_cols],
                            rhs=codes[:, x_cols].bitcast(FP8X4),
                            rhs_scale=scales[:, x_cols],
                            start=(g == 0),
                            stop=(g == PASSES - 1),
                        )

        def add_and_store(unit):
            b, kind = unit // KINDS, unit % KINDS
            g_out, j = kind // PACK, kind % PACK
            if j == 0:
                result[b, g_out] = results.tile([P, WINDOWS, PACK, CHANNELS], F32, name="result")
            res = result[b, g_out]
            for h in range(HEADS):
                channels = slice(h * HEAD_DIM, (h + 1) * HEAD_DIM)
                nc.vector.scalar_tensor_tensor(
                    out=res[:, :, j, channels],
                    in0=sums[unit, h // 2][:, h % 2, :].rearrange("p (n d) -> p n d", n=WINDOWS),
                    scalar=bias_column(h, g_out, j),
                    in1=x_tokens(b)[:, :, g_out, j, channels],
                    op0=ALU.add,
                    op1=ALU.add,
                )
            if j == PACK - 1:
                for n in range(WINDOWS):
                    nc.sync.dma_start(
                        out=out_cut[b, n // 2, n % 2, g_out], in_=res[:, n].rearrange("p j c -> p (j c)")
                    )

        def last_of_batch(i):
            return 0 <= i < TILES and i % WINDOWS == WINDOWS - 1

        for step in range(-STATS_LEAD, UNITS + OUT_LAG):
            if last_of_batch(step + STATS_LEAD - 2):
                inverse_deviation((step + STATS_LEAD - 2) // WINDOWS)
            if 0 <= step - OUT_LAG:
                add_and_store(step - OUT_LAG)
            if last_of_batch(step - QUANT_LAG):
                quantise_tokens((step - QUANT_LAG) // WINDOWS)
            if 0 <= step - 1 < CHUNKS:
                quantise_weights(step - 1)
            if last_of_batch(step + STATS_LEAD - 1):
                root((step + STATS_LEAD - 1) // WINDOWS)
            if 0 <= step - BACK_LAG < TILES:
                to_tokens(step - BACK_LAG)
            if 0 <= step - TURN_LAG < TILES:
                to_channels(step - TURN_LAG)
            if 0 <= step < CHUNKS:
                turn_weights(step)
            if 0 <= step - MIX_LAG < UNITS:
                multiply(step - MIX_LAG)
            if 0 <= step < TILES:
                normalise(step)
            if step + STATS_LEAD < TILES:
                tile_statistics(step + STATS_LEAD)
                if last_of_batch(step + STATS_LEAD):
                    deviation((step + STATS_LEAD) // WINDOWS)
            chunk = step + LOAD_LEAD
            if 0 <= chunk < CHUNKS:
                load_weights(chunk)
                first = TILES_PER_IMAGE + TILES_PER_LOAD * chunk
                for i in range(first, min(first + TILES_PER_LOAD, TILES)):
                    load_tile(i)
